import numpy as np
import ml_dtypes


def mxq(x, axis, fmt="e4m3"):
    dtype, down = {"e4m3": (ml_dtypes.float8_e4m3fn, 7), "e5m2": (ml_dtypes.float8_e5m2, 14)}[fmt]
    v = np.moveaxis(np.asarray(x, np.float32).astype(ml_dtypes.bfloat16).astype(np.float64), axis, -1)
    blocks = v.reshape(v.shape[:-1] + (-1, 32))
    amax = np.abs(blocks).max(-1, keepdims=True)
    byte = np.maximum(np.where(amax > 0, np.frexp(amax)[1] - 1 + 127, 0) - down, 1)
    scale = np.exp2(byte - 127.0)
    codes = (blocks / scale).astype(np.float32).astype(dtype).astype(np.float64)
    return np.moveaxis((codes * scale).reshape(v.shape), -1, axis)


WIDE = False


def mx_kscale(k):
    if not WIDE:
        return np.ones(k)
    levels = np.array([10, -10, 5, -5, 0])
    if k % 512:
        return np.exp2(np.random.permutation(np.resize(levels, k // 32))).repeat(32)
    a = np.empty((k // 512, 16))
    for p in range(k // 512):
        a[p, :8] = np.random.permutation(np.resize(levels, 8))
        for g in range(8):
            far = levels[np.abs(levels - a[p, g]) >= 10]
            a[p, g + 8] = far[np.random.randint(len(far))]
    return np.exp2(a.ravel()).repeat(32)


BF16 = ml_dtypes.bfloat16


def bf(x):
    return np.asarray(x, np.float32).astype(BF16)


def f64(x):
    return np.asarray(x).astype(np.float64)


M, N, NFEAT, NHID, NCLASS = 2048, 2048, 512, 512, 8
ADJ_P = 0.01
SIG = 4.5


def draw0():
    s = mx_kscale(NHID)
    t = mx_kscale(NHID)
    c = np.sqrt(2.0 * SIG / np.sqrt(NHID)) / np.sqrt(NHID)
    return {"h": bf(np.maximum(np.random.standard_normal((N, NHID)), 0.0) * s[None, :]),
            "adj": bf(np.random.uniform(size=(N, N)) < ADJ_P),
            "Qw": bf(np.random.standard_normal((NHID, NHID)) * c / s[:, None] * t[None, :]),
            "Qb": bf(np.random.standard_normal(NHID) * 0.1 * t),
            "Kw": bf(np.random.standard_normal((NHID, NHID)) * c / s[:, None] / t[None, :]),
            "Kb": bf(np.random.standard_normal(NHID) * 0.1 / t)}


def core(h, adj, Qw, Qb, Kw, Kb):
    hq = mxq(f64(h), 1, "e4m3")
    q = (hq @ mxq(f64(Qw), 0, "e4m3")) + f64(Qb)
    k = (hq @ mxq(f64(Kw), 0, "e4m3")) + f64(Kb)
    sc = f64(adj) * (mxq(q, 1, "e4m3") @ mxq(k, 1, "e4m3").T)
    e = np.exp(sc - sc.max(axis=1, keepdims=True))
    return e / e.sum(axis=1, keepdims=True)


def e4m3fn_bytes(y):
    return np.clip(np.asarray(y, np.float64), -448.0, 448.0).astype(np.float32).astype(ml_dtypes.float8_e4m3fn).view(np.uint8)


def e4m3fn_values(b):
    return np.asarray(b, np.uint8).view(ml_dtypes.float8_e4m3fn).astype(np.float64)


def setup_inputs():
    d = draw0()
    x0 = np.asarray(d['h']).astype(np.float64)
    s = (np.max(np.abs(x0), axis=(0,), keepdims=True) / 448.0).astype(np.float32)
    out = {}
    for k, v in d.items():
        if k == 'h':
            out['h_bytes'] = e4m3fn_bytes(x0 / s.astype(np.float64))
            out['h_scale'] = s
        else:
            out[k] = v
    return out


def reference(h_bytes, h_scale, adj, Qw, Qb, Kw, Kb):
    return core(e4m3fn_values(h_bytes) * h_scale.astype(np.float64), adj, Qw, Qb, Kw, Kb)

@@ -1,0 +1,294 @@
+from contextlib import ExitStack
+
+import concourse.mybir as mybir
+from concourse.masks import make_identity
+
+N, D = 2048, 512
+P = 128
+CH = 512
+NCH = N // CH
+T = 4
+ROWS = N // P
+FLOPS = 2 * (2 * N * D * D) + 2 * N * N * D
+
+F32 = mybir.dt.float32
+BF16 = mybir.dt.bfloat16
+U32 = mybir.dt.uint32
+U8 = mybir.dt.uint8
+FP8 = mybir.dt.float8_e4m3fn
+FP8X4 = mybir.dt.float8_e4m3fn_x4
+ALU = mybir.AluOpType
+ACT = mybir.ActivationFunctionType
+
+ADJ_BUFS = 12
+
+
+def tile_gtransformerblock_pb_kernel(tc, h_bytes, h_scale, adj, Qw, Qb, Kw, Kb, out):
+    nc = tc.nc
+    with ExitStack() as ctx:
+        keep = ctx.enter_context(tc.tile_pool(name="keep", bufs=1))
+        work = ctx.enter_context(tc.tile_pool(name="work", bufs=2))
+        adjp = ctx.enter_context(tc.tile_pool(name="adjp", bufs=ADJ_BUFS))
+        rows = ctx.enter_context(tc.tile_pool(name="rows", bufs=4))
+        stats = ctx.enter_context(tc.tile_pool(name="stats", bufs=6))
+        psum = ctx.enter_context(tc.psum_pool(name="psum", bufs=8))
+
+        ident = keep.tile([P, P], F32, name="ident")
+        make_identity(nc, ident[:])
+        ctx.enter_context(tc.manual_schedule())
+
+        scale_b = keep.tile([P, D], F32, name="scale_b")
+        nc.scalar.dma_start(out=scale_b[:], in_=h_scale.rearrange("o k -> (o k)").partition_broadcast(P))
+        warm = keep.tile([P, 1], F32, name="warm")
+        nc.vector.memset(warm[:], 0.0)
+        warm_out = keep.tile([P, 1], F32, name="warm_out")
+        nc.scalar.activation(out=warm_out[:], in_=warm[:], func=ACT.Exp)
+        bias = {}
+        for name, ap in (("k", Kb), ("q", Qb)):
+            bias[name] = keep.tile([P, T], BF16, name="bias_" + name)
+            nc.gpsimd.dma_start(out=bias[name][:], in_=ap.rearrange("(p t) -> p t", t=T))
+
+        hbytes = [keep.tile([P, 4, D], U8, name=f"hbytes{c}") for c in range(NCH)]
+        w_raw = {}
+
+        def load_h(c):
+            nc.sync.dma_start(out=hbytes[c][:], in_=h_bytes[c * CH : (c + 1) * CH, :].rearrange("(p i) k -> p i k", i=4))
+
+        def load_w(name, ap):
+            w_raw[name] = keep.tile([P, T, D], BF16, name="w_raw_" + name)
+            nc.sync.dma_start(out=w_raw[name][:], in_=ap.rearrange("(p j) n -> p j n", j=T))
+
+        load_w("k", Kw)
+        load_h(0)
+        load_h(1)
+        load_h(2)
+        load_h(3)
+        load_w("q", Qw)
+        adj_t = [None] * ROWS
+
+        def load_adj(r):
+            a = adjp.tile([P, N], BF16, name="adj")
+            nc.sync.dma_start(out=a[:], in_=adj[r * P : (r + 1) * P, :])
+            adj_t[r] = a
+
+        for r in range(ADJ_BUFS):
+            load_adj(r)
+
+        def codes(prefix, width):
+            return (
+                keep.tile([P, width], U32, name=prefix + "_codes", align_bytes=64),
+                keep.tile([P, width], U8, name=prefix + "_scales", align_bytes=64),
+            )
+
+        w_q = {name: codes("w" + name, D) for name in ("k", "q")}
+        h_q = [codes(f"h{c}", CH) for c in range(NCH)]
+        x_q = {name: [codes(f"{name}{c}", CH) for c in range(NCH)] for name in ("k", "q")}
+
+        w_grp = {}
+
+        def w_copy(name):
+            w_grp[name] = work.tile([P, D * T], BF16, name="w_grp", align_bytes=64)
+            nc.scalar.copy(
+                out=w_grp[name][:].rearrange("p (t m j) -> p t m j", t=T, j=T),
+                in_=w_raw[name][:].rearrange("p j (m t) -> p t m j", t=T),
+            )
+
+        def w_quant(name):
+            c, s = w_q[name]
+            nc.vector.quantize_mx(out=c[:].bitcast(FP8X4), scales=s[:], in_=w_grp[name][:])
+
+        hb_t = [None] * NCH
+
+        def h_mult(c):
+            hb = work.tile([P, 4, D], BF16, name="hb", align_bytes=64)
+            for i in range(4):
+                nc.vector.tensor_tensor(out=hb[:, i, :], in0=hbytes[c][:, i, :].bitcast(FP8), in1=scale_b[:], op=ALU.mult)
+            hb_t[c] = hb
+
+        hg_t = [None] * NCH
+
+        def h_turn(c):
+            hg = work.tile([P, CH * T], BF16, name="hg", align_bytes=64)
+            words = hg[:].bitcast(F32).rearrange("p (r i u) -> p r i u", i=4, u=2)
+            for half in range(2):
+                xt = psum.tile([P, 2, 2, P], F32, name="ps")
+                for i in range(2):
+                    src = hb_t[c][:, 2 * half + i, :].bitcast(F32)
+                    for u in range(2):
+                        nc.tensor.transpose(xt[:, i, u, :], src[:, u : D // 2 : 2], ident[:])
+                nc.scalar.copy(out=words[:, :, 2 * half : 2 * half + 2, :], in_=xt[:].rearrange("p i u r -> p r i u"))
+            hg_t[c] = hg
+
+        def h_quant(c):
+            cc, s = h_q[c]
+            nc.vector.quantize_mx(out=cc[:].bitcast(FP8X4), scales=s[:], in_=hg_t[c][:])
+
+        stage_t = {}
+        inter_t = {}
+
+        def project(name, c):
+            st = work.tile([P, T, CH], BF16, name="stage", align_bytes=64)
+            for t in range(T):
+                ps = psum.tile([P, CH], F32, name="ps")
+                nc.tensor.matmul_mx(
+                    out=ps[:],
+                    lhsT=w_q[name][0][:, t * P : (t + 1) * P].bitcast(FP8X4),
+                    lhsT_scale=w_q[name][1][:, t * P : (t + 1) * P],
+                    rhs=h_q[c][0][:].bitcast(FP8X4),
+                    rhs_scale=h_q[c][1][:],
+                    start=True,
+                    stop=True,
+                )
+                nc.scalar.activation(out=st[:, t, :], in_=ps[:], func=ACT.Identity, bias=bias[name][:, t : t + 1])
+            stage_t[name, c] = st
+
+        def interleave(name, c):
+            it = work.tile([P, CH, T], BF16, name="inter", align_bytes=64)
+            nc.vector.tensor_copy(out=it[:], in_=stage_t[name, c][:].rearrange("p t n -> p n t"))
+            inter_t[name, c] = it
+
+        def x_quant(name, c):
+            cc, s = x_q[name][c]
+            nc.vector.quantize_mx(out=cc[:].bitcast(FP8X4), scales=s[:], in_=inter_t[name, c][:].rearrange("p n t -> p (n t)"))
+
+        sc_t = [None] * ROWS
+        scb_t = [None] * ROWS
+        e_t = [None] * ROWS
+        nm_t = [None] * ROWS
+        ss_t = [None] * ROWS
+        ri_t = [None] * ROWS
+
+        def scores(r, b):
+            ps = psum.tile([P, CH], F32, name="ps")
+            cols = slice((r % 4) * P, (r % 4 + 1) * P)
+            nc.tensor.matmul_mx(
+                out=ps[:],
+                lhsT=x_q["q"][r // 4][0][:, cols].bitcast(FP8X4),
+                lhsT_scale=x_q["q"][r // 4][1][:, cols],
+                rhs=x_q["k"][b][0][:].bitcast(FP8X4),
+                rhs_scale=x_q["k"][b][1][:],
+                start=True,
+                stop=True,
+            )
+            seg = slice(b * CH, (b + 1) * CH)
+            nc.vector.tensor_tensor(out=sc_t[r][:, seg], in0=ps[:], in1=adj_t[r][:, seg], op=ALU.mult)
+
+        def open_row(r):
+            sc = rows.tile([P, N], F32, name="sc")
+            scb = rows.tile([P, N], BF16, name="scb")
+            sc_t[r] = sc
+            scb_t[r] = scb
+
+        def cast_g(r, b0, b1):
+            seg = slice(b0 * CH, b1 * CH)
+            nc.gpsimd.tensor_scalar(out=scb_t[r][:, seg], in0=sc_t[r][:, seg], scalar1=1.0, scalar2=0.0, op0=ALU.mult, op1=ALU.add)
+
+        def cast_s(r, b0, b1):
+            seg = slice(b0 * CH, b1 * CH)
+            nc.scalar.copy(out=scb_t[r][:, seg], in_=sc_t[r][:, seg])
+
+        def row_max(r):
+            nm = stats.tile([P, 1], F32, name="nm")
+            nc.vector.tensor_scalar(
+                out=scb_t[r][:], in0=scb_t[r][:], scalar1=-1.0, scalar2=None, op0=ALU.mult, op1=ALU.min, accum_out=nm[:]
+            )
+            nm_t[r] = nm
+
+        def row_exp(r):
+            e = rows.tile([P, N], F32, name="e")
+            ss = stats.tile([P, 1], F32, name="ss")
+            nc.scalar.activation(out=e[:], in_=sc_t[r][:], func=ACT.Exp, bias=nm_t[r][:], accum_out=ss[:])
+            e_t[r] = e
+            ss_t[r] = ss
+
+        def row_recip(r):
+            ri = stats.tile([P, 1], F32, name="ri")
+            nc.vector.reciprocal(out=ri[:], in_=ss_t[r][:])
+            ri_t[r] = ri
+
+        def norm_g(r, a, b):
+            nc.gpsimd.tensor_scalar(out=e_t[r][:, a:b], in0=e_t[r][:, a:b], scalar1=ri_t[r][:], scalar2=0.0, op0=ALU.mult, op1=ALU.add)
+
+        def norm_v(r, a, b):
+            nc.vector.tensor_scalar(out=e_t[r][:, a:b], in0=e_t[r][:, a:b], scalar1=ri_t[r][:], scalar2=None, op0=ALU.mult)
+
+        def norm_s(r, a, b):
+            nc.scalar.activation(out=e_t[r][:, a:b], in_=e_t[r][:, a:b], func=ACT.Copy, scale=ri_t[r][:])
+
+        def store(r, a, b):
+            nc.sync.dma_start(out=out[r * P : (r + 1) * P, a:b], in_=e_t[r][:, a:b])
+
+        w_copy("k")
+        h_mult(0)
+        h_turn(0)
+        h_mult(1)
+        w_quant("k")
+        h_turn(1)
+        h_quant(0)
+        w_copy("q")
+        h_mult(2)
+        project("k", 0)
+        h_quant(1)
+        h_turn(2)
+        h_mult(3)
+        project("k", 1)
+        interleave("k", 0)
+        w_quant("q")
+        h_turn(3)
+        h_quant(2)
+        x_quant("k", 0)
+        project("k", 2)
+        interleave("k", 1)
+        h_quant(3)
+        x_quant("k", 1)
+        project("q", 0)
+        interleave("k", 2)
+        project("k", 3)
+        x_quant("k", 2)
+        interleave("q", 0)
+        x_quant("q", 0)
+        open_row(0)
+        scores(0, 0)
+        scores(0, 1)
+        interleave("k", 3)
+        scores(0, 2)
+        x_quant("k", 3)
+
+        LAST = ROWS - 1
+        for r in range(ROWS + 1):
+            chunk = (r + 3) // 4
+            if r % 4 == 1 and chunk < NCH:
+                project("q", chunk)
+            if r < ROWS:
+                if r > 0:
+                    open_row(r)
+                for b in range(3 if r == 0 else 0, NCH):
+                    scores(r, b)
+            if r % 4 == 2 and chunk < NCH:
+                interleave("q", chunk)
+            if r >= 2:
+                row_exp(r - 2)
+            if r >= 3:
+                norm_g(r - 3, 0, N)
+                store(r - 3, 0, N)
+                if r - 3 + ADJ_BUFS < ROWS:
+                    load_adj(r - 3 + ADJ_BUFS)
+            if r < ROWS:
+                cast_g(r, 0, 1)
+                cast_g(r, 1, 2)
+                cast_s(r, 2, 4)
+            if r >= 1:
+                row_max(r - 1)
+            if r % 4 == 2 and chunk < NCH:
+                x_quant("q", chunk)
+            if r >= 2:
+                row_recip(r - 2)
+        row_exp(LAST)
+        norm_g(LAST - 1, 0, N)
+        store(LAST - 1, 0, N)
+        row_recip(LAST)
+        norm_s(LAST, 0, 512)
+        norm_g(LAST, 512, 1024)
+        norm_v(LAST, 1024, 2048)
+        store(LAST, 0, 1024)
+        store(LAST, 1024, 2048)

@@ -20,7 +20,8 @@ FP8X4 = mybir.dt.float8_e4m3fn_x4
 ALU = mybir.AluOpType
 ACT = mybir.ActivationFunctionType
 
-ADJ_BUFS = 12
+ADJ_BUFS = 8
+SC_BUFS = 5
 
 
 def tile_gtransformerblock_pb_kernel(tc, h_bytes, h_scale, adj, Qw, Qb, Kw, Kb, out):
@@ -30,15 +31,14 @@ def tile_gtransformerblock_pb_kernel(tc, h_bytes, h_scale, adj, Qw, Qb, Kw, Kb, 
         work = ctx.enter_context(tc.tile_pool(name="work", bufs=2))
         adjp = ctx.enter_context(tc.tile_pool(name="adjp", bufs=ADJ_BUFS))
         rows = ctx.enter_context(tc.tile_pool(name="rows", bufs=4))
-        stats = ctx.enter_context(tc.tile_pool(name="stats", bufs=6))
+        scp = ctx.enter_context(tc.tile_pool(name="scp", bufs=SC_BUFS))
+        stats = ctx.enter_context(tc.tile_pool(name="stats", bufs=8))
         psum = ctx.enter_context(tc.psum_pool(name="psum", bufs=8))
 
         ident = keep.tile([P, P], F32, name="ident")
         make_identity(nc, ident[:])
         ctx.enter_context(tc.manual_schedule())
 
-        scale_b = keep.tile([P, D], F32, name="scale_b")
-        nc.scalar.dma_start(out=scale_b[:], in_=h_scale.rearrange("o k -> (o k)").partition_broadcast(P))
         warm = keep.tile([P, 1], F32, name="warm")
         nc.vector.memset(warm[:], 0.0)
         warm_out = keep.tile([P, 1], F32, name="warm_out")
@@ -59,11 +59,13 @@ def tile_gtransformerblock_pb_kernel(tc, h_bytes, h_scale, adj, Qw, Qb, Kw, Kb, 
             nc.sync.dma_start(out=w_raw[name][:], in_=ap.rearrange("(p j) n -> p j n", j=T))
 
         load_w("k", Kw)
+        scale_b = keep.tile([P, D], F32, name="scale_b")
+        nc.sync.dma_start(out=scale_b[:], in_=h_scale.rearrange("o k -> (o k)").partition_broadcast(P))
         load_h(0)
+        load_w("q", Qw)
         load_h(1)
         load_h(2)
         load_h(3)
-        load_w("q", Qw)
         adj_t = [None] * ROWS
 
         def load_adj(r):
@@ -86,11 +88,12 @@ def tile_gtransformerblock_pb_kernel(tc, h_bytes, h_scale, adj, Qw, Qb, Kw, Kb, 
 
         w_grp = {}
 
-        def w_copy(name):
-            w_grp[name] = work.tile([P, D * T], BF16, name="w_grp", align_bytes=64)
-            nc.scalar.copy(
-                out=w_grp[name][:].rearrange("p (t m j) -> p t m j", t=T, j=T),
-                in_=w_raw[name][:].rearrange("p j (m t) -> p t m j", t=T),
+        def w_copy(name, eng, t0=0, t1=T):
+            if t0 == 0:
+                w_grp[name] = work.tile([P, D * T], BF16, name="w_grp", align_bytes=64)
+            eng(
+                out=w_grp[name][:].rearrange("p (t m j) -> p t m j", t=T, j=T)[:, t0:t1],
+                in_=w_raw[name][:].rearrange("p j (m t) -> p t m j", t=T)[:, t0:t1],
             )
 
         def w_quant(name):
@@ -127,7 +130,7 @@ def tile_gtransformerblock_pb_kernel(tc, h_bytes, h_scale, adj, Qw, Qb, Kw, Kb, 
         inter_t = {}
 
         def project(name, c):
-            st = work.tile([P, T, CH], BF16, name="stage", align_bytes=64)
+            st = work.tile([P, T, CH], BF16, name="stage", bufs=4, align_bytes=64)
             for t in range(T):
                 ps = psum.tile([P, CH], F32, name="ps")
                 nc.tensor.matmul_mx(
@@ -142,9 +145,9 @@ def tile_gtransformerblock_pb_kernel(tc, h_bytes, h_scale, adj, Qw, Qb, Kw, Kb, 
                 nc.scalar.activation(out=st[:, t, :], in_=ps[:], func=ACT.Identity, bias=bias[name][:, t : t + 1])
             stage_t[name, c] = st
 
-        def interleave(name, c):
+        def interleave(name, c, eng=nc.vector.tensor_copy):
             it = work.tile([P, CH, T], BF16, name="inter", align_bytes=64)
-            nc.vector.tensor_copy(out=it[:], in_=stage_t[name, c][:].rearrange("p t n -> p n t"))
+            eng(out=it[:].rearrange("p (c i) t -> p c t i", i=4), in_=stage_t[name, c][:].rearrange("p t (c i) -> p c t i", i=4))
             inter_t[name, c] = it
 
         def x_quant(name, c):
@@ -174,8 +177,8 @@ def tile_gtransformerblock_pb_kernel(tc, h_bytes, h_scale, adj, Qw, Qb, Kw, Kb, 
             nc.vector.tensor_tensor(out=sc_t[r][:, seg], in0=ps[:], in1=adj_t[r][:, seg], op=ALU.mult)
 
         def open_row(r):
-            sc = rows.tile([P, N], F32, name="sc")
-            scb = rows.tile([P, N], BF16, name="scb")
+            sc = scp.tile([P, N], F32, name="sc")
+            scb = scp.tile([P, N], BF16, name="scb", bufs=3)
             sc_t[r] = sc
             scb_t[r] = scb
 
@@ -194,8 +197,28 @@ def tile_gtransformerblock_pb_kernel(tc, h_bytes, h_scale, adj, Qw, Qb, Kw, Kb, 
             )
             nm_t[r] = nm
 
+        def reduce_max(r):
+            mx = stats.tile([P, 1], F32, name="mx")
+            nc.vector.tensor_reduce(out=mx[:], in_=sc_t[r][:], axis=mybir.AxisListType.X, op=ALU.max)
+            nm = stats.tile([P, 1], F32, name="nm")
+            nc.vector.tensor_scalar(out=nm[:], in0=mx[:], scalar1=-1.0, scalar2=None, op0=ALU.mult)
+            nm_t[r] = nm
+
+        hf_t = [None] * ROWS
+
+        def fold_max(r):
+            hf = work.tile([P, N // 2], BF16, name="hf", bufs=1)
+            nc.vector.tensor_tensor(out=hf[:], in0=sc_t[r][:, : N // 2], in1=sc_t[r][:, N // 2 :], op=ALU.max)
+            hf_t[r] = hf
+
+        def fold_acc(r):
+            nm = stats.tile([P, 1], F32, name="nm")
+            hf = hf_t[r]
+            nc.vector.tensor_scalar(out=hf[:], in0=hf[:], scalar1=-1.0, scalar2=None, op0=ALU.mult, op1=ALU.min, accum_out=nm[:])
+            nm_t[r] = nm
+
         def row_exp(r):
-            e = rows.tile([P, N], F32, name="e")
+            e = rows.tile([P, N], F32, name="e", bufs=5)
             ss = stats.tile([P, 1], F32, name="ss")
             nc.scalar.activation(out=e[:], in_=sc_t[r][:], func=ACT.Exp, bias=nm_t[r][:], accum_out=ss[:])
             e_t[r] = e
@@ -218,77 +241,82 @@ def tile_gtransformerblock_pb_kernel(tc, h_bytes, h_scale, adj, Qw, Qb, Kw, Kb, 
         def store(r, a, b):
             nc.sync.dma_start(out=out[r * P : (r + 1) * P, a:b], in_=e_t[r][:, a:b])
 
-        w_copy("k")
+        VC = nc.vector.tensor_copy
+        SC = nc.scalar.copy
+        w_copy("k", VC)
+        w_quant("k")
         h_mult(0)
         h_turn(0)
+        w_copy("q", SC)
         h_mult(1)
-        w_quant("k")
-        h_turn(1)
         h_quant(0)
-        w_copy("q")
-        h_mult(2)
+        h_turn(1)
         project("k", 0)
+        h_mult(2)
         h_quant(1)
-        h_turn(2)
-        h_mult(3)
         project("k", 1)
-        interleave("k", 0)
         w_quant("q")
+        h_turn(2)
+        interleave("k", 0)
+        h_mult(3)
+        x_quant("k", 0)
+        project("q", 0)
         h_turn(3)
         h_quant(2)
-        x_quant("k", 0)
-        project("k", 2)
         interleave("k", 1)
+        project("k", 2)
         h_quant(3)
         x_quant("k", 1)
-        project("q", 0)
-        interleave("k", 2)
-        project("k", 3)
-        x_quant("k", 2)
         interleave("q", 0)
+        project("k", 3)
         x_quant("q", 0)
-        open_row(0)
-        scores(0, 0)
-        scores(0, 1)
+        project("q", 1)
+        interleave("k", 2)
+        project("q", 2)
+        x_quant("k", 2)
         interleave("k", 3)
-        scores(0, 2)
+        project("q", 3)
         x_quant("k", 3)
-
         LAST = ROWS - 1
-        for r in range(ROWS + 1):
-            chunk = (r + 3) // 4
-            if r % 4 == 1 and chunk < NCH:
-                project("q", chunk)
-            if r < ROWS:
-                if r > 0:
-                    open_row(r)
-                for b in range(3 if r == 0 else 0, NCH):
-                    scores(r, b)
-            if r % 4 == 2 and chunk < NCH:
-                interleave("q", chunk)
-            if r >= 2:
+        for r in range(ROWS):
+            last = r == LAST
+            open_row(r)
+            cg = 0 if last else 1 + (r % 3 == 0)
+            if r > 1:
                 row_exp(r - 2)
-            if r >= 3:
-                norm_g(r - 3, 0, N)
-                store(r - 3, 0, N)
-                if r - 3 + ADJ_BUFS < ROWS:
-                    load_adj(r - 3 + ADJ_BUFS)
-            if r < ROWS:
-                cast_g(r, 0, 1)
-                cast_g(r, 1, 2)
-                cast_s(r, 2, 4)
-            if r >= 1:
-                row_max(r - 1)
-            if r % 4 == 2 and chunk < NCH:
-                x_quant("q", chunk)
-            if r >= 2:
+            for b in range(4):
+                scores(r, b)
+                if b < cg:
+                    cast_g(r, b, b + 1)
+                if b == (1 if last else 3) and r > 0:
+                    row_max(r - 1)
+            for q in (1, 2, 3):
+                if r == (0, 1, 2)[q - 1]:
+                    interleave("q", q)
+                    x_quant("q", q)
+            if not last:
+                cast_s(r, cg, 4)
+            if r > 1 and not last:
                 row_recip(r - 2)
+                norm_g(r - 2, 0, 1024)
+                norm_g(r - 2, 1024, N)
+                store(r - 2, 0, N)
+            if r + 8 < ROWS:
+                load_adj(r + 8)
+        row_exp(LAST - 1)
+        row_recip(LAST - 2)
+        norm_v(LAST - 2, 0, N)
+        store(LAST - 2, 0, N)
+        fold_max(LAST)
+        fold_acc(LAST)
         row_exp(LAST)
-        norm_g(LAST - 1, 0, N)
+        row_recip(LAST - 1)
+        norm_v(LAST - 1, 0, N)
         store(LAST - 1, 0, N)
         row_recip(LAST)
-        norm_s(LAST, 0, 512)
-        norm_g(LAST, 512, 1024)
-        norm_v(LAST, 1024, 2048)
-        store(LAST, 0, 1024)
-        store(LAST, 1024, 2048)
+        norm_s(LAST, 1536, N)
+        norm_v(LAST, 0, 768)
+        store(LAST, 0, 768)
+        norm_v(LAST, 768, 1536)
+        store(LAST, 768, 1536)
+        store(LAST, 1536, N)

@@ -9,6 +9,7 @@ CH = 512
 NCH = N // CH
 T = 4
 ROWS = N // P
+LAST = ROWS - 1
 FLOPS = 2 * (2 * N * D * D) + 2 * N * N * D
 
 F32 = mybir.dt.float32
@@ -21,7 +22,6 @@ ALU = mybir.AluOpType
 ACT = mybir.ActivationFunctionType
 
 ADJ_BUFS = 8
-SC_BUFS = 5
 
 
 def tile_gtransformerblock_pb_kernel(tc, h_bytes, h_scale, adj, Qw, Qb, Kw, Kb, out):
@@ -31,7 +31,7 @@ def tile_gtransformerblock_pb_kernel(tc, h_bytes, h_scale, adj, Qw, Qb, Kw, Kb, 
         work = ctx.enter_context(tc.tile_pool(name="work", bufs=2))
         adjp = ctx.enter_context(tc.tile_pool(name="adjp", bufs=ADJ_BUFS))
         rows = ctx.enter_context(tc.tile_pool(name="rows", bufs=4))
-        scp = ctx.enter_context(tc.tile_pool(name="scp", bufs=SC_BUFS))
+        scp = ctx.enter_context(tc.tile_pool(name="scp", bufs=5))
         stats = ctx.enter_context(tc.tile_pool(name="stats", bufs=8))
         psum = ctx.enter_context(tc.psum_pool(name="psum", bufs=8))
 
@@ -150,6 +150,28 @@ def tile_gtransformerblock_pb_kernel(tc, h_bytes, h_scale, adj, Qw, Qb, Kw, Kb, 
             eng(out=it[:].rearrange("p (c i) t -> p c t i", i=4), in_=stage_t[name, c][:].rearrange("p t (c i) -> p c t i", i=4))
             inter_t[name, c] = it
 
+        def direct(name, c):
+            it = work.tile([P, CH, T], BF16, name="inter", align_bytes=64)
+            for g in range(4):
+                ps = psum.tile([P, T, P], F32, name="ps")
+                for t in range(T):
+                    nc.tensor.matmul_mx(
+                        out=ps[:, t, :],
+                        lhsT=w_q[name][0][:, t * P : (t + 1) * P].bitcast(FP8X4),
+                        lhsT_scale=w_q[name][1][:, t * P : (t + 1) * P],
+                        rhs=h_q[c][0][:, g * P : (g + 1) * P].bitcast(FP8X4),
+                        rhs_scale=h_q[c][1][:, g * P : (g + 1) * P],
+                        start=True,
+                        stop=True,
+                    )
+                nc.vector.tensor_tensor(
+                    out=it[:, g * P : (g + 1) * P, :],
+                    in0=ps[:].rearrange("p t n -> p n t"),
+                    in1=bias[name][:].unsqueeze(1).to_broadcast([P, P, T]),
+                    op=ALU.add,
+                )
+            inter_t[name, c] = it
+
         def x_quant(name, c):
             cc, s = x_q[name][c]
             nc.vector.quantize_mx(out=cc[:].bitcast(FP8X4), scales=s[:], in_=inter_t[name, c][:].rearrange("p n t -> p (n t)"))
@@ -197,13 +219,6 @@ def tile_gtransformerblock_pb_kernel(tc, h_bytes, h_scale, adj, Qw, Qb, Kw, Kb, 
             )
             nm_t[r] = nm
 
-        def reduce_max(r):
-            mx = stats.tile([P, 1], F32, name="mx")
-            nc.vector.tensor_reduce(out=mx[:], in_=sc_t[r][:], axis=mybir.AxisListType.X, op=ALU.max)
-            nm = stats.tile([P, 1], F32, name="nm")
-            nc.vector.tensor_scalar(out=nm[:], in0=mx[:], scalar1=-1.0, scalar2=None, op0=ALU.mult)
-            nm_t[r] = nm
-
         hf_t = [None] * ROWS
 
         def fold_max(r):
@@ -244,79 +259,81 @@ def tile_gtransformerblock_pb_kernel(tc, h_bytes, h_scale, adj, Qw, Qb, Kw, Kb, 
         VC = nc.vector.tensor_copy
         SC = nc.scalar.copy
         w_copy("k", VC)
-        w_quant("k")
+        w_copy("q", SC)
         h_mult(0)
         h_turn(0)
-        w_copy("q", SC)
+        w_quant("k")
         h_mult(1)
         h_quant(0)
         h_turn(1)
         project("k", 0)
-        h_mult(2)
-        h_quant(1)
-        project("k", 1)
         w_quant("q")
-        h_turn(2)
-        interleave("k", 0)
-        h_mult(3)
-        x_quant("k", 0)
         project("q", 0)
-        h_turn(3)
-        h_quant(2)
-        interleave("k", 1)
-        project("k", 2)
-        h_quant(3)
-        x_quant("k", 1)
-        interleave("q", 0)
-        project("k", 3)
+        h_quant(1)
+        h_mult(2)
+        interleave("q", 0, SC)
+        h_mult(3)
+        direct("k", 1)
         x_quant("q", 0)
-        project("q", 1)
-        interleave("k", 2)
-        project("q", 2)
-        x_quant("k", 2)
-        interleave("k", 3)
-        project("q", 3)
+        h_turn(2)
+        h_quant(2)
+        x_quant("k", 1)
+        h_turn(3)
+        interleave("k", 0, SC)
+        h_quant(3)
+        x_quant("k", 0)
+        project("k", 2)
+        direct("k", 3)
         x_quant("k", 3)
-        LAST = ROWS - 1
+        interleave("k", 2, SC)
+        x_quant("k", 2)
         for r in range(ROWS):
-            last = r == LAST
             open_row(r)
-            cg = 0 if last else 1 + (r % 3 == 0)
+            cg = 0 if r == LAST else 2 if r < 8 else 1
             if r > 1:
                 row_exp(r - 2)
             for b in range(4):
                 scores(r, b)
                 if b < cg:
                     cast_g(r, b, b + 1)
-                if b == (1 if last else 3) and r > 0:
+                if r > 0 and b == (1 if r == LAST else 3):
                     row_max(r - 1)
-            for q in (1, 2, 3):
-                if r == (0, 1, 2)[q - 1]:
-                    interleave("q", q)
-                    x_quant("q", q)
-            if not last:
+            if r == 0:
+                project("q", 1)
+            elif r == 1:
+                interleave("q", 1, SC)
+                x_quant("q", 1)
+            elif r == 5:
+                project("q", 2)
+                direct("q", 3)
+            elif r == 6:
+                interleave("q", 2, SC)
+                x_quant("q", 2)
+            elif r == 9:
+                x_quant("q", 3)
+            if r < LAST:
                 cast_s(r, cg, 4)
-            if r > 1 and not last:
-                row_recip(r - 2)
-                norm_g(r - 2, 0, 1024)
-                norm_g(r - 2, 1024, N)
-                store(r - 2, 0, N)
-            if r + 8 < ROWS:
-                load_adj(r + 8)
+                if r > 1:
+                    row_recip(r - 2)
+                    norm_g(r - 2, 0, 1024)
+                    norm_g(r - 2, 1024, N)
+                    store(r - 2, 0, N)
+            if r + ADJ_BUFS < ROWS:
+                load_adj(r + ADJ_BUFS)
         row_exp(LAST - 1)
         row_recip(LAST - 2)
         norm_v(LAST - 2, 0, N)
-        store(LAST - 2, 0, N)
         fold_max(LAST)
+        row_recip(LAST - 1)
+        store(LAST - 2, 0, N)
         fold_acc(LAST)
         row_exp(LAST)
-        row_recip(LAST - 1)
         norm_v(LAST - 1, 0, N)
-        store(LAST - 1, 0, N)
         row_recip(LAST)
-        norm_s(LAST, 1536, N)
         norm_v(LAST, 0, 768)
-        store(LAST, 0, 768)
-        norm_v(LAST, 768, 1536)
-        store(LAST, 768, 1536)
+        store(LAST - 1, 0, N)
+        norm_s(LAST, 1536, N)
         store(LAST, 1536, N)
+        norm_v(LAST, 768, 1536)
+        store(LAST, 0, 768)
+        store(LAST, 768, 1536)

@@ -30,8 +30,7 @@ def tile_gtransformerblock_pb_kernel(tc, h_bytes, h_scale, adj, Qw, Qb, Kw, Kb, 
         keep = ctx.enter_context(tc.tile_pool(name="keep", bufs=1))
         work = ctx.enter_context(tc.tile_pool(name="work", bufs=2))
         adjp = ctx.enter_context(tc.tile_pool(name="adjp", bufs=ADJ_BUFS))
-        rows = ctx.enter_context(tc.tile_pool(name="rows", bufs=4))
-        scp = ctx.enter_context(tc.tile_pool(name="scp", bufs=5))
+        rows = ctx.enter_context(tc.tile_pool(name="rows", bufs=5))
         stats = ctx.enter_context(tc.tile_pool(name="stats", bufs=8))
         psum = ctx.enter_context(tc.psum_pool(name="psum", bufs=8))
 
@@ -39,40 +38,43 @@ def tile_gtransformerblock_pb_kernel(tc, h_bytes, h_scale, adj, Qw, Qb, Kw, Kb, 
         make_identity(nc, ident[:])
         ctx.enter_context(tc.manual_schedule())
 
+        scale_row = keep.tile([P, D], F32, name="scale_row")
+        nc.vector.memset(scale_row[:], 0.0)
         warm = keep.tile([P, 1], F32, name="warm")
         nc.vector.memset(warm[:], 0.0)
+        ones = keep.tile([P, P], F32, name="ones")
+        nc.vector.memset(ones[:], 1.0)
         warm_out = keep.tile([P, 1], F32, name="warm_out")
         nc.scalar.activation(out=warm_out[:], in_=warm[:], func=ACT.Exp)
+        ident_b = keep.tile([P, P], BF16, name="ident_b")
+        nc.scalar.copy(out=ident_b[:], in_=ident[:])
         bias = {}
         for name, ap in (("k", Kb), ("q", Qb)):
             bias[name] = keep.tile([P, T], BF16, name="bias_" + name)
             nc.gpsimd.dma_start(out=bias[name][:], in_=ap.rearrange("(p t) -> p t", t=T))
 
-        hbytes = [keep.tile([P, 4, D], U8, name=f"hbytes{c}") for c in range(NCH)]
-        w_raw = {}
+        h_raw = [keep.tile([P, 4, D], U8, name=f"h_raw{c}") for c in range(NCH)]
+        w_raw = {name: keep.tile([P, T, D], BF16, name="w_raw_" + name) for name in ("k", "q")}
 
         def load_h(c):
-            nc.sync.dma_start(out=hbytes[c][:], in_=h_bytes[c * CH : (c + 1) * CH, :].rearrange("(p i) k -> p i k", i=4))
+            nc.sync.dma_start(out=h_raw[c][:], in_=h_bytes[c * CH : (c + 1) * CH, :].rearrange("(p i) k -> p i k", i=4))
 
         def load_w(name, ap):
-            w_raw[name] = keep.tile([P, T, D], BF16, name="w_raw_" + name)
             nc.sync.dma_start(out=w_raw[name][:], in_=ap.rearrange("(p j) n -> p j n", j=T))
 
-        load_w("k", Kw)
-        scale_b = keep.tile([P, D], F32, name="scale_b")
-        nc.sync.dma_start(out=scale_b[:], in_=h_scale.rearrange("o k -> (o k)").partition_broadcast(P))
-        load_h(0)
-        load_w("q", Qw)
-        load_h(1)
-        load_h(2)
-        load_h(3)
-        adj_t = [None] * ROWS
+        adj_t = {}
 
         def load_adj(r):
             a = adjp.tile([P, N], BF16, name="adj")
             nc.sync.dma_start(out=a[:], in_=adj[r * P : (r + 1) * P, :])
             adj_t[r] = a
 
+        load_w("k", Kw)
+        nc.sync.dma_start(out=scale_row[0:1, :], in_=h_scale[:, :])
+        load_h(0)
+        load_w("q", Qw)
+        for c in range(1, NCH):
+            load_h(c)
         for r in range(ADJ_BUFS):
             load_adj(r)
 
@@ -86,254 +88,304 @@ def tile_gtransformerblock_pb_kernel(tc, h_bytes, h_scale, adj, Qw, Qb, Kw, Kb, 
         h_q = [codes(f"h{c}", CH) for c in range(NCH)]
         x_q = {name: [codes(f"{name}{c}", CH) for c in range(NCH)] for name in ("k", "q")}
 
-        w_grp = {}
+        def quantise(dst, src):
+            nc.vector.quantize_mx(out=dst[0][:].bitcast(FP8X4), scales=dst[1][:], in_=src[:])
 
-        def w_copy(name, eng, t0=0, t1=T):
-            if t0 == 0:
-                w_grp[name] = work.tile([P, D * T], BF16, name="w_grp", align_bytes=64)
-            eng(
-                out=w_grp[name][:].rearrange("p (t m j) -> p t m j", t=T, j=T)[:, t0:t1],
-                in_=w_raw[name][:].rearrange("p j (m t) -> p t m j", t=T)[:, t0:t1],
-            )
-
-        def w_quant(name):
-            c, s = w_q[name]
-            nc.vector.quantize_mx(out=c[:].bitcast(FP8X4), scales=s[:], in_=w_grp[name][:])
-
-        hb_t = [None] * NCH
-
-        def h_mult(c):
-            hb = work.tile([P, 4, D], BF16, name="hb", align_bytes=64)
-            for i in range(4):
-                nc.vector.tensor_tensor(out=hb[:, i, :], in0=hbytes[c][:, i, :].bitcast(FP8), in1=scale_b[:], op=ALU.mult)
-            hb_t[c] = hb
-
-        hg_t = [None] * NCH
-
-        def h_turn(c):
-            hg = work.tile([P, CH * T], BF16, name="hg", align_bytes=64)
-            words = hg[:].bitcast(F32).rearrange("p (r i u) -> p r i u", i=4, u=2)
-            for half in range(2):
-                xt = psum.tile([P, 2, 2, P], F32, name="ps")
-                for i in range(2):
-                    src = hb_t[c][:, 2 * half + i, :].bitcast(F32)
-                    for u in range(2):
-                        nc.tensor.transpose(xt[:, i, u, :], src[:, u : D // 2 : 2], ident[:])
-                nc.scalar.copy(out=words[:, :, 2 * half : 2 * half + 2, :], in_=xt[:].rearrange("p i u r -> p r i u"))
-            hg_t[c] = hg
-
-        def h_quant(c):
-            cc, s = h_q[c]
-            nc.vector.quantize_mx(out=cc[:].bitcast(FP8X4), scales=s[:], in_=hg_t[c][:])
-
-        stage_t = {}
-        inter_t = {}
-
-        def project(name, c):
-            st = work.tile([P, T, CH], BF16, name="stage", bufs=4, align_bytes=64)
-            for t in range(T):
-                ps = psum.tile([P, CH], F32, name="ps")
-                nc.tensor.matmul_mx(
-                    out=ps[:],
-                    lhsT=w_q[name][0][:, t * P : (t + 1) * P].bitcast(FP8X4),
-                    lhsT_scale=w_q[name][1][:, t * P : (t + 1) * P],
-                    rhs=h_q[c][0][:].bitcast(FP8X4),
-                    rhs_scale=h_q[c][1][:],
-                    start=True,
-                    stop=True,
-                )
-                nc.scalar.activation(out=st[:, t, :], in_=ps[:], func=ACT.Identity, bias=bias[name][:, t : t + 1])
-            stage_t[name, c] = st
-
-        def interleave(name, c, eng=nc.vector.tensor_copy):
-            it = work.tile([P, CH, T], BF16, name="inter", align_bytes=64)
-            eng(out=it[:].rearrange("p (c i) t -> p c t i", i=4), in_=stage_t[name, c][:].rearrange("p t (c i) -> p c t i", i=4))
-            inter_t[name, c] = it
-
-        def direct(name, c):
-            it = work.tile([P, CH, T], BF16, name="inter", align_bytes=64)
-            for g in range(4):
-                ps = psum.tile([P, T, P], F32, name="ps")
-                for t in range(T):
-                    nc.tensor.matmul_mx(
-                        out=ps[:, t, :],
-                        lhsT=w_q[name][0][:, t * P : (t + 1) * P].bitcast(FP8X4),
-                        lhsT_scale=w_q[name][1][:, t * P : (t + 1) * P],
-                        rhs=h_q[c][0][:, g * P : (g + 1) * P].bitcast(FP8X4),
-                        rhs_scale=h_q[c][1][:, g * P : (g + 1) * P],
-                        start=True,
-                        stop=True,
-                    )
-                nc.vector.tensor_tensor(
-                    out=it[:, g * P : (g + 1) * P, :],
-                    in0=ps[:].rearrange("p t n -> p n t"),
-                    in1=bias[name][:].unsqueeze(1).to_broadcast([P, P, T]),
-                    op=ALU.add,
-                )
-            inter_t[name, c] = it
-
-        def x_quant(name, c):
-            cc, s = x_q[name][c]
-            nc.vector.quantize_mx(out=cc[:].bitcast(FP8X4), scales=s[:], in_=inter_t[name, c][:].rearrange("p n t -> p (n t)"))
-
-        sc_t = [None] * ROWS
-        scb_t = [None] * ROWS
-        e_t = [None] * ROWS
-        nm_t = [None] * ROWS
-        ss_t = [None] * ROWS
-        ri_t = [None] * ROWS
-
-        def scores(r, b):
-            ps = psum.tile([P, CH], F32, name="ps")
-            cols = slice((r % 4) * P, (r % 4 + 1) * P)
+        def matmul_mx(dst, stationary, cols, moving):
             nc.tensor.matmul_mx(
-                out=ps[:],
-                lhsT=x_q["q"][r // 4][0][:, cols].bitcast(FP8X4),
-                lhsT_scale=x_q["q"][r // 4][1][:, cols],
-                rhs=x_q["k"][b][0][:].bitcast(FP8X4),
-                rhs_scale=x_q["k"][b][1][:],
+                out=dst[:],
+                lhsT=stationary[0][:, cols].bitcast(FP8X4),
+                lhsT_scale=stationary[1][:, cols],
+                rhs=moving[0][:].bitcast(FP8X4),
+                rhs_scale=moving[1][:],
                 start=True,
                 stop=True,
             )
-            seg = slice(b * CH, (b + 1) * CH)
-            nc.vector.tensor_tensor(out=sc_t[r][:, seg], in0=ps[:], in1=adj_t[r][:, seg], op=ALU.mult)
+
+        COPY = {"V": nc.vector.tensor_copy, "S": nc.scalar.copy}
+
+        def block(i):
+            return slice(i * P, (i + 1) * P)
+
+        def banks(b, n):
+            return slice(b * CH, (b + n) * CH)
+
+        scale_ps = psum.tile([P, D], F32, name="ps")
+        nc.tensor.matmul(out=scale_ps[:], lhsT=ones[:], rhs=scale_row[:], start=True, stop=True)
+        scale_b = keep.tile([P, D], F32, name="scale_b")
+        nc.scalar.copy(out=scale_b[:], in_=scale_ps[:])
+
+        w_grp = {}
+
+        def new_w_grp(name):
+            w_grp[name] = work.tile([P, T * D], BF16, name="w_grp", align_bytes=64)
+            return w_grp[name], w_raw[name][:].rearrange("p j (m t) -> p t m j", t=T)
+
+        def w_copy(name):
+            g, src = new_w_grp(name)
+            nc.vector.tensor_copy(out=g[:].rearrange("p (t m j) -> p t m j", t=T, j=T), in_=src)
+
+        def via_identity(dst, sources, eng):
+            ps = psum.tile([P, 2 * CH], BF16, name="ps")
+            for i, src in enumerate(sources):
+                nc.tensor.matmul(out=ps[:, banks(i, 1)], lhsT=ident_b[:], rhs=src, start=True, stop=True)
+            COPY[eng](out=dst, in_=ps[:])
+
+        def w_copy_pe(name):
+            g, src = new_w_grp(name)
+            for half in range(2):
+                via_identity(g[:, banks(2 * half, 2)], [src[:, 2 * half], src[:, 2 * half + 1]], "S")
+
+        def w_quant(name):
+            quantise(w_q[name], w_grp[name])
+
+        h_val = {}
+        h_grp = {}
+
+        def h_mult(c):
+            hv = work.tile([P, 4, D], BF16, name="h_val", align_bytes=64)
+            for i in range(4):
+                nc.vector.tensor_tensor(out=hv[:, i, :], in0=h_raw[c][:, i, :].bitcast(FP8), in1=scale_b[:], op=ALU.mult)
+            h_val[c] = hv
+
+        def h_turn(c):
+            hg = work.tile([P, CH * T], BF16, name="h_grp", align_bytes=64)
+            words = hg[:].bitcast(F32).rearrange("p (r i u) -> p r i u", i=4, u=2)
+            for half in range(2):
+                ps = psum.tile([P, 2, 2, P], F32, name="ps")
+                for i in range(2):
+                    src = h_val[c][:, 2 * half + i, :].bitcast(F32)
+                    for u in range(2):
+                        nc.tensor.transpose(ps[:, i, u, :], src[:, u : D // 2 : 2], ident[:])
+                nc.scalar.copy(out=words[:, :, 2 * half : 2 * half + 2, :], in_=ps[:].rearrange("p i u r -> p r i u"))
+            h_grp[c] = hg
+
+        def h_quant(c):
+            quantise(h_q[c], h_grp[c])
+
+        stage = {}
+        inter = {}
+
+        def project(name, c, engines="SSSS"):
+            st = work.tile([P, T, CH], BF16, name="stage", bufs=3, align_bytes=64)
+            for t in range(T):
+                ps = psum.tile([P, CH], F32, name="ps")
+                matmul_mx(ps, w_q[name], block(t), h_q[c])
+                b = bias[name][:, t : t + 1]
+                if engines[t] == "S":
+                    nc.scalar.activation(out=st[:, t, :], in_=ps[:], func=ACT.Identity, bias=b)
+                else:
+                    nc.vector.tensor_scalar(out=st[:, t, :], in0=ps[:], scalar1=b, scalar2=None, op0=ALU.add)
+            stage[name, c] = st
+
+        def new_inter(name, c):
+            inter[name, c] = work.tile([P, CH * T], BF16, name="inter", align_bytes=64)
+            return inter[name, c]
+
+        def interleave(name, c):
+            it = new_inter(name, c)
+            nc.vector.tensor_copy(out=it[:].rearrange("p (n t) -> p n t", t=T), in_=stage[name, c][:].rearrange("p t n -> p n t"))
+
+        def interleave_g(name, c):
+            it = new_inter(name, c)
+            nc.gpsimd.tensor_scalar(
+                out=it[:].rearrange("p (n t) -> p n t", t=T),
+                in0=stage[name, c][:].rearrange("p t n -> p n t"),
+                scalar1=1.0,
+                scalar2=0.0,
+                op0=ALU.mult,
+                op1=ALU.add,
+            )
+
+        def interleave_pe(name, c, engines):
+            it = new_inter(name, c)
+            for half in range(2):
+                src = [stage[name, c][:, :, block(2 * half + i)].rearrange("p t n -> p n t") for i in range(2)]
+                via_identity(it[:, banks(2 * half, 2)], src, engines[half])
+
+        def x_quant(name, c):
+            quantise(x_q[name][c], inter[name, c])
+
+        sc = {}
+        sc_bf = {}
+        folded = {}
+        neg_max = {}
+        e = {}
+        e_sum = {}
+        inv = {}
+
+        def scores(r, b):
+            ps = psum.tile([P, CH], F32, name="ps")
+            matmul_mx(ps, x_q["q"][r // 4], block(r % 4), x_q["k"][b])
+            nc.vector.tensor_tensor(out=sc[r][:, banks(b, 1)], in0=ps[:], in1=adj_t[r][:, banks(b, 1)], op=ALU.mult)
 
         def open_row(r):
-            sc = scp.tile([P, N], F32, name="sc")
-            scb = scp.tile([P, N], BF16, name="scb", bufs=3)
-            sc_t[r] = sc
-            scb_t[r] = scb
+            sc_r = rows.tile([P, N], F32, name="sc")
+            sc[r] = sc_r
+            neg_max[r] = stats.tile([P, 2], F32, name="neg_max")
+            if r < LAST:
+                sc_bf[r] = rows.tile([P, N], BF16, name="sc_bf", bufs=3)
 
-        def cast_g(r, b0, b1):
-            seg = slice(b0 * CH, b1 * CH)
-            nc.gpsimd.tensor_scalar(out=scb_t[r][:, seg], in0=sc_t[r][:, seg], scalar1=1.0, scalar2=0.0, op0=ALU.mult, op1=ALU.add)
+        def cast_g(r, b):
+            nc.gpsimd.tensor_scalar(
+                out=sc_bf[r][:, banks(b, 1)], in0=sc[r][:, banks(b, 1)], scalar1=1.0, scalar2=0.0, op0=ALU.mult, op1=ALU.add
+            )
 
-        def cast_s(r, b0, b1):
-            seg = slice(b0 * CH, b1 * CH)
-            nc.scalar.copy(out=scb_t[r][:, seg], in_=sc_t[r][:, seg])
+        def cast_s(r, b):
+            nc.scalar.copy(out=sc_bf[r][:, b * CH :], in_=sc[r][:, b * CH :])
+
+        def max_of(x, nm):
+            nc.vector.tensor_scalar(out=x, in0=x, scalar1=-1.0, scalar2=None, op0=ALU.mult, op1=ALU.min, accum_out=nm)
 
         def row_max(r):
-            nm = stats.tile([P, 1], F32, name="nm")
-            nc.vector.tensor_scalar(
-                out=scb_t[r][:], in0=scb_t[r][:], scalar1=-1.0, scalar2=None, op0=ALU.mult, op1=ALU.min, accum_out=nm[:]
+            max_of(sc_bf[r][:], neg_max[r][:, 0:1])
+
+        def fold(r, half):
+            folded[r, half] = work.tile([P, CH], BF16, name="folded", bufs=1)
+            a = sc[r][:, banks(2 * half, 1)]
+            b = sc[r][:, banks(2 * half + 1, 1)]
+            nc.vector.tensor_tensor(out=folded[r, half][:], in0=a, in1=b, op=ALU.max)
+
+        def fold_max(r, half):
+            max_of(folded[r, half][:], neg_max[r][:, half : half + 1])
+
+        def row_exp(r, half=None):
+            if not half:
+                e[r] = rows.tile([P, N], F32, name="e")
+                e_sum[r] = stats.tile([P, 2], F32, name="e_sum")
+            seg, col = (slice(0, N), 0) if half is None else (banks(2 * half, 2), half)
+            nc.scalar.activation(
+                out=e[r][:, seg],
+                in_=sc[r][:, seg],
+                func=ACT.Exp,
+                bias=neg_max[r][:, col : col + 1],
+                accum_out=e_sum[r][:, col : col + 1],
             )
-            nm_t[r] = nm
 
-        hf_t = [None] * ROWS
+        def row_recip(r, total=None):
+            inv[r] = stats.tile([P, 1], F32, name="inv")
+            nc.vector.reciprocal(out=inv[r][:], in_=e_sum[r][:, 0:1] if total is None else total)
 
-        def fold_max(r):
-            hf = work.tile([P, N // 2], BF16, name="hf", bufs=1)
-            nc.vector.tensor_tensor(out=hf[:], in0=sc_t[r][:, : N // 2], in1=sc_t[r][:, N // 2 :], op=ALU.max)
-            hf_t[r] = hf
+        def norm_g(r, b, n):
+            x = e[r][:, banks(b, n)]
+            nc.gpsimd.tensor_scalar(out=x, in0=x, scalar1=inv[r][:], scalar2=0.0, op0=ALU.mult, op1=ALU.add)
 
-        def fold_acc(r):
-            nm = stats.tile([P, 1], F32, name="nm")
-            hf = hf_t[r]
-            nc.vector.tensor_scalar(out=hf[:], in0=hf[:], scalar1=-1.0, scalar2=None, op0=ALU.mult, op1=ALU.min, accum_out=nm[:])
-            nm_t[r] = nm
+        def norm_v(r, b, n):
+            x = e[r][:, banks(b, n)]
+            nc.vector.tensor_scalar(out=x, in0=x, scalar1=inv[r][:], scalar2=None, op0=ALU.mult)
 
-        def row_exp(r):
-            e = rows.tile([P, N], F32, name="e", bufs=5)
-            ss = stats.tile([P, 1], F32, name="ss")
-            nc.scalar.activation(out=e[:], in_=sc_t[r][:], func=ACT.Exp, bias=nm_t[r][:], accum_out=ss[:])
-            e_t[r] = e
-            ss_t[r] = ss
+        def store(r, b, n):
+            nc.sync.dma_start(out=out[r * P : (r + 1) * P, banks(b, n)], in_=e[r][:, banks(b, n)])
 
-        def row_recip(r):
-            ri = stats.tile([P, 1], F32, name="ri")
-            nc.vector.reciprocal(out=ri[:], in_=ss_t[r][:])
-            ri_t[r] = ri
-
-        def norm_g(r, a, b):
-            nc.gpsimd.tensor_scalar(out=e_t[r][:, a:b], in0=e_t[r][:, a:b], scalar1=ri_t[r][:], scalar2=0.0, op0=ALU.mult, op1=ALU.add)
-
-        def norm_v(r, a, b):
-            nc.vector.tensor_scalar(out=e_t[r][:, a:b], in0=e_t[r][:, a:b], scalar1=ri_t[r][:], scalar2=None, op0=ALU.mult)
-
-        def norm_s(r, a, b):
-            nc.scalar.activation(out=e_t[r][:, a:b], in_=e_t[r][:, a:b], func=ACT.Copy, scale=ri_t[r][:])
-
-        def store(r, a, b):
-            nc.sync.dma_start(out=out[r * P : (r + 1) * P, a:b], in_=e_t[r][:, a:b])
-
-        VC = nc.vector.tensor_copy
-        SC = nc.scalar.copy
-        w_copy("k", VC)
-        w_copy("q", SC)
+        w_copy_pe("q")
+        w_copy("k")
+        w_quant("k")
         h_mult(0)
         h_turn(0)
-        w_quant("k")
         h_mult(1)
         h_quant(0)
+        w_quant("q")
         h_turn(1)
         project("k", 0)
-        w_quant("q")
-        project("q", 0)
-        h_quant(1)
         h_mult(2)
-        interleave("q", 0, SC)
         h_mult(3)
-        direct("k", 1)
-        x_quant("q", 0)
+        h_quant(1)
+        project("q", 0)
         h_turn(2)
+        interleave_pe("k", 0, "VS")
+        interleave("q", 0)
         h_quant(2)
-        x_quant("k", 1)
         h_turn(3)
-        interleave("k", 0, SC)
+        project("k", 1, "VSSV")
         h_quant(3)
         x_quant("k", 0)
-        project("k", 2)
-        direct("k", 3)
-        x_quant("k", 3)
-        interleave("k", 2, SC)
+        project("k", 2, "VSSS")
+        interleave("k", 1)
+        x_quant("q", 0)
+        project("k", 3)
+        interleave_pe("k", 2, "SS")
+        x_quant("k", 1)
+        interleave("k", 3)
+        project("q", 1)
         x_quant("k", 2)
+        x_quant("k", 3)
+
         for r in range(ROWS):
+            on_g = 0 if r == LAST else 3 if r < 2 else 2 if r % 3 == 2 else 1
             open_row(r)
-            cg = 0 if r == LAST else 2 if r < 8 else 1
             if r > 1:
                 row_exp(r - 2)
             for b in range(4):
                 scores(r, b)
-                if b < cg:
-                    cast_g(r, b, b + 1)
-                if r > 0 and b == (1 if r == LAST else 3):
-                    row_max(r - 1)
+                if b < on_g:
+                    cast_g(r, b)
+                if r == 0 and b == 1:
+                    project("q", 2)
+            if r > 0:
+                row_max(r - 1)
             if r == 0:
-                project("q", 1)
+                interleave_g("q", 1)
             elif r == 1:
-                interleave("q", 1, SC)
+                project("q", 3)
+            elif r == 2:
+                interleave_pe("q", 2, "VS")
                 x_quant("q", 1)
-            elif r == 5:
-                project("q", 2)
-                direct("q", 3)
             elif r == 6:
-                interleave("q", 2, SC)
+                interleave_pe("q", 3, "VS")
+            elif r == 7:
                 x_quant("q", 2)
-            elif r == 9:
                 x_quant("q", 3)
             if r < LAST:
-                cast_s(r, cg, 4)
+                cast_s(r, on_g)
                 if r > 1:
                     row_recip(r - 2)
-                    norm_g(r - 2, 0, 1024)
-                    norm_g(r - 2, 1024, N)
-                    store(r - 2, 0, N)
+                    norm_g(r - 2, 0, 2)
+                    norm_g(r - 2, 2, 2)
+                    store(r - 2, 0, 4)
             if r + ADJ_BUFS < ROWS:
                 load_adj(r + ADJ_BUFS)
-        row_exp(LAST - 1)
+
+        fold(LAST, 0)
         row_recip(LAST - 2)
-        norm_v(LAST - 2, 0, N)
-        fold_max(LAST)
+        norm_v(LAST - 2, 0, 2)
+        row_exp(LAST - 1)
+        fold_max(LAST, 0)
+        norm_v(LAST - 2, 2, 2)
+        store(LAST - 2, 0, 2)
+        store(LAST - 2, 2, 2)
+        fold(LAST, 1)
         row_recip(LAST - 1)
-        store(LAST - 2, 0, N)
-        fold_acc(LAST)
-        row_exp(LAST)
-        norm_v(LAST - 1, 0, N)
-        row_recip(LAST)
-        norm_v(LAST, 0, 768)
-        store(LAST - 1, 0, N)
-        norm_s(LAST, 1536, N)
-        store(LAST, 1536, N)
-        norm_v(LAST, 768, 1536)
-        store(LAST, 0, 768)
-        store(LAST, 768, 1536)
+        fold_max(LAST, 1)
+        norm_v(LAST - 1, 0, 2)
+        store(LAST - 1, 0, 2)
+        row_exp(LAST, 0)
+        row_exp(LAST, 1)
+        last_neg = stats.tile([P, 1], F32, name="last_neg")
+        nc.vector.tensor_tensor(out=last_neg[:], in0=neg_max[LAST][:, 0:1], in1=neg_max[LAST][:, 1:2], op=ALU.min)
+        norm_v(LAST - 1, 2, 2)
+        store(LAST - 1, 2, 2)
+        weight = stats.tile([P, 2], F32, name="weight")
+        nc.scalar.activation(out=weight[:], in_=neg_max[LAST][:], func=ACT.Exp, scale=-1.0, bias=last_neg[:])
+        weighted = stats.tile([P, 2], F32, name="weighted")
+        total = stats.tile([P, 1], F32, name="total")
+        nc.vector.scalar_tensor_tensor(
+            out=weighted[:], in0=e_sum[LAST][:], scalar=1.0, in1=weight[:], op0=ALU.mult, op1=ALU.mult, accum_out=total[:]
+        )
+        row_recip(LAST, total[:])
+        factor = stats.tile([P, 2], F32, name="factor")
+        nc.vector.tensor_scalar(out=factor[:], in0=weight[:], scalar1=inv[LAST][:], scalar2=None, op0=ALU.mult)
+
+        def norm_last(eng, b, n):
+            x = e[LAST][:, banks(b, n)]
+            f = factor[:, b // 2 : b // 2 + 1]
+            if eng == "S":
+                nc.scalar.activation(out=x, in_=x, func=ACT.Copy, scale=f)
+            else:
+                nc.vector.tensor_scalar(out=x, in0=x, scalar1=f, scalar2=None, op0=ALU.mult)
+
+        norm_last("S", 3, 1)
+        norm_last("V", 2, 1)
+        store(LAST, 2, 1)
+        norm_last("V", 0, 2)
+        store(LAST, 3, 1)
+        store(LAST, 0, 2)

@@ -22,6 +22,7 @@ ALU = mybir.AluOpType
 ACT = mybir.ActivationFunctionType
 
 ADJ_BUFS = 8
+EARLY = 4
 
 
 def tile_gtransformerblock_pb_kernel(tc, h_bytes, h_scale, adj, Qw, Qb, Kw, Kb, out):
@@ -102,7 +103,10 @@ def tile_gtransformerblock_pb_kernel(tc, h_bytes, h_scale, adj, Qw, Qb, Kw, Kb, 
                 stop=True,
             )
 
-        COPY = {"V": nc.vector.tensor_copy, "S": nc.scalar.copy}
+        def gpsimd_copy(out, in_):
+            nc.gpsimd.tensor_scalar(out=out, in0=in_, scalar1=1.0, scalar2=0.0, op0=ALU.mult, op1=ALU.add)
+
+        COPY = {"V": nc.vector.tensor_copy, "S": nc.scalar.copy, "G": gpsimd_copy}
 
         def block(i):
             return slice(i * P, (i + 1) * P)
@@ -110,31 +114,27 @@ def tile_gtransformerblock_pb_kernel(tc, h_bytes, h_scale, adj, Qw, Qb, Kw, Kb, 
         def banks(b, n):
             return slice(b * CH, (b + n) * CH)
 
-        scale_ps = psum.tile([P, D], F32, name="ps")
-        nc.tensor.matmul(out=scale_ps[:], lhsT=ones[:], rhs=scale_row[:], start=True, stop=True)
+        HALVES = (slice(0, D // 2), slice(D // 2, D))
         scale_b = keep.tile([P, D], F32, name="scale_b")
-        nc.scalar.copy(out=scale_b[:], in_=scale_ps[:])
+        for cols in HALVES:
+            ps = psum.tile([P, D // 2], F32, name="ps")
+            nc.tensor.matmul(out=ps[:], lhsT=ones[:], rhs=scale_row[:, cols], start=True, stop=True)
+            nc.scalar.copy(out=scale_b[:, cols], in_=ps[:])
 
         w_grp = {}
 
-        def new_w_grp(name):
-            w_grp[name] = work.tile([P, T * D], BF16, name="w_grp", align_bytes=64)
-            return w_grp[name], w_raw[name][:].rearrange("p j (m t) -> p t m j", t=T)
-
-        def w_copy(name):
-            g, src = new_w_grp(name)
-            nc.vector.tensor_copy(out=g[:].rearrange("p (t m j) -> p t m j", t=T, j=T), in_=src)
+        def w_copy(name, eng):
+            g = work.tile([P, T * D], BF16, name="w_grp", align_bytes=64)
+            COPY[eng](
+                out=g[:].rearrange("p (t m j) -> p t m j", t=T, j=T), in_=w_raw[name][:].rearrange("p j (m t) -> p t m j", t=T)
+            )
+            w_grp[name] = g
 
         def via_identity(dst, sources, eng):
             ps = psum.tile([P, 2 * CH], BF16, name="ps")
             for i, src in enumerate(sources):
                 nc.tensor.matmul(out=ps[:, banks(i, 1)], lhsT=ident_b[:], rhs=src, start=True, stop=True)
             COPY[eng](out=dst, in_=ps[:])
-
-        def w_copy_pe(name):
-            g, src = new_w_grp(name)
-            for half in range(2):
-                via_identity(g[:, banks(2 * half, 2)], [src[:, 2 * half], src[:, 2 * half + 1]], "S")
 
         def w_quant(name):
             quantise(w_q[name], w_grp[name])
@@ -144,11 +144,14 @@ def tile_gtransformerblock_pb_kernel(tc, h_bytes, h_scale, adj, Qw, Qb, Kw, Kb, 
 
         def h_mult(c):
             hv = work.tile([P, 4, D], BF16, name="h_val", align_bytes=64)
-            for i in range(4):
-                nc.vector.tensor_tensor(out=hv[:, i, :], in0=h_raw[c][:, i, :].bitcast(FP8), in1=scale_b[:], op=ALU.mult)
+            for cols in HALVES if c == 0 else (slice(0, D),):
+                for i in range(4):
+                    nc.vector.tensor_tensor(
+                        out=hv[:, i, cols], in0=h_raw[c][:, i, cols].bitcast(FP8), in1=scale_b[:, cols], op=ALU.mult
+                    )
             h_val[c] = hv
 
-        def h_turn(c):
+        def h_turn(c, engines="SS"):
             hg = work.tile([P, CH * T], BF16, name="h_grp", align_bytes=64)
             words = hg[:].bitcast(F32).rearrange("p (r i u) -> p r i u", i=4, u=2)
             for half in range(2):
@@ -157,7 +160,7 @@ def tile_gtransformerblock_pb_kernel(tc, h_bytes, h_scale, adj, Qw, Qb, Kw, Kb, 
                     src = h_val[c][:, 2 * half + i, :].bitcast(F32)
                     for u in range(2):
                         nc.tensor.transpose(ps[:, i, u, :], src[:, u : D // 2 : 2], ident[:])
-                nc.scalar.copy(out=words[:, :, 2 * half : 2 * half + 2, :], in_=ps[:].rearrange("p i u r -> p r i u"))
+                COPY[engines[half]](out=words[:, :, 2 * half : 2 * half + 2, :], in_=ps[:].rearrange("p i u r -> p r i u"))
             h_grp[c] = hg
 
         def h_quant(c):
@@ -182,20 +185,9 @@ def tile_gtransformerblock_pb_kernel(tc, h_bytes, h_scale, adj, Qw, Qb, Kw, Kb, 
             inter[name, c] = work.tile([P, CH * T], BF16, name="inter", align_bytes=64)
             return inter[name, c]
 
-        def interleave(name, c):
+        def interleave(name, c, eng):
             it = new_inter(name, c)
-            nc.vector.tensor_copy(out=it[:].rearrange("p (n t) -> p n t", t=T), in_=stage[name, c][:].rearrange("p t n -> p n t"))
-
-        def interleave_g(name, c):
-            it = new_inter(name, c)
-            nc.gpsimd.tensor_scalar(
-                out=it[:].rearrange("p (n t) -> p n t", t=T),
-                in0=stage[name, c][:].rearrange("p t n -> p n t"),
-                scalar1=1.0,
-                scalar2=0.0,
-                op0=ALU.mult,
-                op1=ALU.add,
-            )
+            COPY[eng](out=it[:].rearrange("p (n t) -> p n t", t=T), in_=stage[name, c][:].rearrange("p t n -> p n t"))
 
         def interleave_pe(name, c, engines):
             it = new_inter(name, c)
@@ -223,16 +215,11 @@ def tile_gtransformerblock_pb_kernel(tc, h_bytes, h_scale, adj, Qw, Qb, Kw, Kb, 
             sc_r = rows.tile([P, N], F32, name="sc")
             sc[r] = sc_r
             neg_max[r] = stats.tile([P, 2], F32, name="neg_max")
-            if r < LAST:
+
+        def cast(r, b, n, eng):
+            if b == 0:
                 sc_bf[r] = rows.tile([P, N], BF16, name="sc_bf", bufs=3)
-
-        def cast_g(r, b):
-            nc.gpsimd.tensor_scalar(
-                out=sc_bf[r][:, banks(b, 1)], in0=sc[r][:, banks(b, 1)], scalar1=1.0, scalar2=0.0, op0=ALU.mult, op1=ALU.add
-            )
-
-        def cast_s(r, b):
-            nc.scalar.copy(out=sc_bf[r][:, b * CH :], in_=sc[r][:, b * CH :])
+            COPY[eng](out=sc_bf[r][:, banks(b, n)], in_=sc[r][:, banks(b, n)])
 
         def max_of(x, nm):
             nc.vector.tensor_scalar(out=x, in0=x, scalar1=-1.0, scalar2=None, op0=ALU.mult, op1=ALU.min, accum_out=nm)
@@ -277,66 +264,72 @@ def tile_gtransformerblock_pb_kernel(tc, h_bytes, h_scale, adj, Qw, Qb, Kw, Kb, 
         def store(r, b, n):
             nc.sync.dma_start(out=out[r * P : (r + 1) * P, banks(b, n)], in_=e[r][:, banks(b, n)])
 
-        w_copy_pe("q")
-        w_copy("k")
+        w_copy("k", "V")
         w_quant("k")
+        w_copy("q", "S")
         h_mult(0)
         h_turn(0)
         h_mult(1)
         h_quant(0)
-        w_quant("q")
         h_turn(1)
         project("k", 0)
+        w_quant("q")
         h_mult(2)
-        h_mult(3)
         h_quant(1)
         project("q", 0)
+        h_mult(3)
         h_turn(2)
+        interleave("q", 0, "V")
         interleave_pe("k", 0, "VS")
-        interleave("q", 0)
         h_quant(2)
-        h_turn(3)
-        project("k", 1, "VSSV")
-        h_quant(3)
         x_quant("k", 0)
-        project("k", 2, "VSSS")
-        interleave("k", 1)
+        h_turn(3)
         x_quant("q", 0)
+        project("k", 1, "SVSS")
+        h_quant(3)
+        project("k", 2, "SVSS")
+        for r in range(EARLY):
+            open_row(r)
+            scores(r, 0)
+        interleave("k", 1, "G")
+        x_quant("k", 1)
         project("k", 3)
         interleave_pe("k", 2, "SS")
-        x_quant("k", 1)
-        interleave("k", 3)
-        project("q", 1)
+        interleave("k", 3, "V")
         x_quant("k", 2)
+        project("q", 1, "SSVS")
         x_quant("k", 3)
 
         for r in range(ROWS):
-            on_g = 0 if r == LAST else 3 if r < 2 else 2 if r % 3 == 2 else 1
-            open_row(r)
+            on_g = 4 if r == 0 else 3 if r < 3 else 0 if r >= LAST - 1 else 2 if r % 3 == 1 else 1
+            if r >= EARLY:
+                open_row(r)
             if r > 1:
                 row_exp(r - 2)
             for b in range(4):
-                scores(r, b)
+                if b > 0 or r >= EARLY:
+                    scores(r, b)
                 if b < on_g:
-                    cast_g(r, b)
-                if r == 0 and b == 1:
+                    cast(r, b, 1, "G")
+                if r > 0 and b == 3:
+                    row_max(r - 1)
+                if (r, b) == (0, 0):
                     project("q", 2)
-            if r > 0:
-                row_max(r - 1)
-            if r == 0:
-                interleave_g("q", 1)
-            elif r == 1:
-                project("q", 3)
-            elif r == 2:
-                interleave_pe("q", 2, "VS")
-                x_quant("q", 1)
-            elif r == 6:
-                interleave_pe("q", 3, "VS")
-            elif r == 7:
-                x_quant("q", 2)
-                x_quant("q", 3)
+                elif (r, b) == (1, 3):
+                    project("q", 3)
+                elif (r, b) == (3, 2):
+                    interleave_pe("q", 1, "VV")
+                    interleave_pe("q", 2, "SS")
+                elif (r, b) == (3, 3):
+                    x_quant("q", 1)
+                    x_quant("q", 2)
+                elif (r, b) == (8, 3):
+                    interleave_pe("q", 3, "VV")
+                elif (r, b) == (9, 3):
+                    x_quant("q", 3)
             if r < LAST:
-                cast_s(r, on_g)
+                if on_g < 4:
+                    cast(r, on_g, 4 - on_g, "S")
                 if r > 1:
                     row_recip(r - 2)
                     norm_g(r - 2, 0, 2)
@@ -347,23 +340,21 @@ def tile_gtransformerblock_pb_kernel(tc, h_bytes, h_scale, adj, Qw, Qb, Kw, Kb, 
 
         fold(LAST, 0)
         row_recip(LAST - 2)
-        norm_v(LAST - 2, 0, 2)
-        row_exp(LAST - 1)
         fold_max(LAST, 0)
+        norm_v(LAST - 2, 0, 2)
         norm_v(LAST - 2, 2, 2)
         store(LAST - 2, 0, 2)
-        store(LAST - 2, 2, 2)
+        row_exp(LAST - 1)
         fold(LAST, 1)
         row_recip(LAST - 1)
         fold_max(LAST, 1)
         norm_v(LAST - 1, 0, 2)
-        store(LAST - 1, 0, 2)
-        row_exp(LAST, 0)
-        row_exp(LAST, 1)
         last_neg = stats.tile([P, 1], F32, name="last_neg")
         nc.vector.tensor_tensor(out=last_neg[:], in0=neg_max[LAST][:, 0:1], in1=neg_max[LAST][:, 1:2], op=ALU.min)
+        row_exp(LAST, 0)
+        store(LAST - 2, 2, 2)
         norm_v(LAST - 1, 2, 2)
-        store(LAST - 1, 2, 2)
+        row_exp(LAST, 1)
         weight = stats.tile([P, 2], F32, name="weight")
         nc.scalar.activation(out=weight[:], in_=neg_max[LAST][:], func=ACT.Exp, scale=-1.0, bias=last_neg[:])
         weighted = stats.tile([P, 2], F32, name="weighted")
@@ -372,20 +363,22 @@ def tile_gtransformerblock_pb_kernel(tc, h_bytes, h_scale, adj, Qw, Qb, Kw, Kb, 
             out=weighted[:], in0=e_sum[LAST][:], scalar=1.0, in1=weight[:], op0=ALU.mult, op1=ALU.mult, accum_out=total[:]
         )
         row_recip(LAST, total[:])
+        store(LAST - 1, 0, 2)
+        store(LAST - 1, 2, 2)
         factor = stats.tile([P, 2], F32, name="factor")
         nc.vector.tensor_scalar(out=factor[:], in0=weight[:], scalar1=inv[LAST][:], scalar2=None, op0=ALU.mult)
 
         def norm_last(eng, b, n):
             x = e[LAST][:, banks(b, n)]
-            f = factor[:, b // 2 : b // 2 + 1]
+            col = slice(b // 2, b // 2 + 1)
             if eng == "S":
-                nc.scalar.activation(out=x, in_=x, func=ACT.Copy, scale=f)
+                nc.scalar.activation(out=x, in_=x, func=ACT.Copy, scale=factor[:, col])
             else:
-                nc.vector.tensor_scalar(out=x, in0=x, scalar1=f, scalar2=None, op0=ALU.mult)
+                nc.vector.tensor_scalar(out=x, in0=x, scalar1=weight[:, col], scalar2=inv[LAST][:], op0=ALU.mult, op1=ALU.mult)
 
-        norm_last("S", 3, 1)
         norm_last("V", 2, 1)
         store(LAST, 2, 1)
+        norm_last("S", 3, 1)
         norm_last("V", 0, 2)
-        store(LAST, 3, 1)
         store(LAST, 0, 2)
+        store(LAST, 3, 1)

from contextlib import ExitStack

import concourse.mybir as mybir
from concourse.masks import make_identity

N, D = 2048, 512
P = 128
CH = 512
NCH = N // CH
T = 4
ROWS = N // P
LAST = ROWS - 1
FLOPS = 2 * (2 * N * D * D) + 2 * N * N * D

F32 = mybir.dt.float32
BF16 = mybir.dt.bfloat16
U32 = mybir.dt.uint32
U8 = mybir.dt.uint8
FP8 = mybir.dt.float8_e4m3fn
FP8X4 = mybir.dt.float8_e4m3fn_x4
ALU = mybir.AluOpType
ACT = mybir.ActivationFunctionType

ADJ_BUFS = 8
EARLY = 4


def tile_gtransformerblock_pb_kernel(tc, h_bytes, h_scale, adj, Qw, Qb, Kw, Kb, out):
    nc = tc.nc
    with ExitStack() as ctx:
        keep = ctx.enter_context(tc.tile_pool(name="keep", bufs=1))
        work = ctx.enter_context(tc.tile_pool(name="work", bufs=2))
        adjp = ctx.enter_context(tc.tile_pool(name="adjp", bufs=ADJ_BUFS))
        rows = ctx.enter_context(tc.tile_pool(name="rows", bufs=5))
        stats = ctx.enter_context(tc.tile_pool(name="stats", bufs=8))
        psum = ctx.enter_context(tc.psum_pool(name="psum", bufs=8))

        ident = keep.tile([P, P], F32, name="ident")
        make_identity(nc, ident[:])
        ctx.enter_context(tc.manual_schedule())

        scale_row = keep.tile([P, D], F32, name="scale_row")
        nc.vector.memset(scale_row[:], 0.0)
        warm = keep.tile([P, 1], F32, name="warm")
        nc.vector.memset(warm[:], 0.0)
        ones = keep.tile([P, P], F32, name="ones")
        nc.vector.memset(ones[:], 1.0)
        warm_out = keep.tile([P, 1], F32, name="warm_out")
        nc.scalar.activation(out=warm_out[:], in_=warm[:], func=ACT.Exp)
        ident_b = keep.tile([P, P], BF16, name="ident_b")
        nc.scalar.copy(out=ident_b[:], in_=ident[:])
        bias = {}
        for name, ap in (("k", Kb), ("q", Qb)):
            bias[name] = keep.tile([P, T], BF16, name="bias_" + name)
            nc.gpsimd.dma_start(out=bias[name][:], in_=ap.rearrange("(p t) -> p t", t=T))

        h_raw = [keep.tile([P, 4, D], U8, name=f"h_raw{c}") for c in range(NCH)]
        w_raw = {name: keep.tile([P, T, D], BF16, name="w_raw_" + name) for name in ("k", "q")}

        def load_h(c):
            nc.sync.dma_start(out=h_raw[c][:], in_=h_bytes[c * CH : (c + 1) * CH, :].rearrange("(p i) k -> p i k", i=4))

        def load_w(name, ap):
            nc.sync.dma_start(out=w_raw[name][:], in_=ap.rearrange("(p j) n -> p j n", j=T))

        adj_t = {}

        def load_adj(r):
            a = adjp.tile([P, N], BF16, name="adj")
            nc.sync.dma_start(out=a[:], in_=adj[r * P : (r + 1) * P, :])
            adj_t[r] = a

        load_w("k", Kw)
        nc.sync.dma_start(out=scale_row[0:1, :], in_=h_scale[:, :])
        load_h(0)
        load_w("q", Qw)
        for c in range(1, NCH):
            load_h(c)
        for r in range(ADJ_BUFS):
            load_adj(r)

        def codes(prefix, width):
            return (
                keep.tile([P, width], U32, name=prefix + "_codes", align_bytes=64),
                keep.tile([P, width], U8, name=prefix + "_scales", align_bytes=64),
            )

        w_q = {name: codes("w" + name, D) for name in ("k", "q")}
        h_q = [codes(f"h{c}", CH) for c in range(NCH)]
        x_q = {name: [codes(f"{name}{c}", CH) for c in range(NCH)] for name in ("k", "q")}

        def quantise(dst, src):
            nc.vector.quantize_mx(out=dst[0][:].bitcast(FP8X4), scales=dst[1][:], in_=src[:])

        def matmul_mx(dst, stationary, cols, moving):
            nc.tensor.matmul_mx(
                out=dst[:],
                lhsT=stationary[0][:, cols].bitcast(FP8X4),
                lhsT_scale=stationary[1][:, cols],
                rhs=moving[0][:].bitcast(FP8X4),
                rhs_scale=moving[1][:],
                start=True,
                stop=True,
            )

        def gpsimd_copy(out, in_):
            nc.gpsimd.tensor_scalar(out=out, in0=in_, scalar1=1.0, scalar2=0.0, op0=ALU.mult, op1=ALU.add)

        COPY = {"V": nc.vector.tensor_copy, "S": nc.scalar.copy, "G": gpsimd_copy}

        def block(i):
            return slice(i * P, (i + 1) * P)

        def banks(b, n):
            return slice(b * CH, (b + n) * CH)

        HALVES = (slice(0, D // 2), slice(D // 2, D))
        scale_b = keep.tile([P, D], F32, name="scale_b")
        for cols in HALVES:
            ps = psum.tile([P, D // 2], F32, name="ps")
            nc.tensor.matmul(out=ps[:], lhsT=ones[:], rhs=scale_row[:, cols], start=True, stop=True)
            nc.scalar.copy(out=scale_b[:, cols], in_=ps[:])

        w_grp = {}

        def w_copy(name, eng):
            g = work.tile([P, T * D], BF16, name="w_grp", align_bytes=64)
            COPY[eng](
                out=g[:].rearrange("p (t m j) -> p t m j", t=T, j=T), in_=w_raw[name][:].rearrange("p j (m t) -> p t m j", t=T)
            )
            w_grp[name] = g

        def via_identity(dst, sources, eng):
            ps = psum.tile([P, 2 * CH], BF16, name="ps")
            for i, src in enumerate(sources):
                nc.tensor.matmul(out=ps[:, banks(i, 1)], lhsT=ident_b[:], rhs=src, start=True, stop=True)
            COPY[eng](out=dst, in_=ps[:])

        def w_quant(name):
            quantise(w_q[name], w_grp[name])

        h_val = {}
        h_grp = {}

        def h_mult(c):
            hv = work.tile([P, 4, D], BF16, name="h_val", align_bytes=64)
            for cols in HALVES if c == 0 else (slice(0, D),):
                for i in range(4):
                    nc.vector.tensor_tensor(
                        out=hv[:, i, cols], in0=h_raw[c][:, i, cols].bitcast(FP8), in1=scale_b[:, cols], op=ALU.mult
                    )
            h_val[c] = hv

        def h_turn(c, engines="SS"):
            hg = work.tile([P, CH * T], BF16, name="h_grp", align_bytes=64)
            words = hg[:].bitcast(F32).rearrange("p (r i u) -> p r i u", i=4, u=2)
            for half in range(2):
                ps = psum.tile([P, 2, 2, P], F32, name="ps")
                for i in range(2):
                    src = h_val[c][:, 2 * half + i, :].bitcast(F32)
                    for u in range(2):
                        nc.tensor.transpose(ps[:, i, u, :], src[:, u : D // 2 : 2], ident[:])
                COPY[engines[half]](out=words[:, :, 2 * half : 2 * half + 2, :], in_=ps[:].rearrange("p i u r -> p r i u"))
            h_grp[c] = hg

        def h_quant(c):
            quantise(h_q[c], h_grp[c])

        stage = {}
        inter = {}

        def project(name, c, engines="SSSS"):
            st = work.tile([P, T, CH], BF16, name="stage", bufs=3, align_bytes=64)
            for t in range(T):
                ps = psum.tile([P, CH], F32, name="ps")
                matmul_mx(ps, w_q[name], block(t), h_q[c])
                b = bias[name][:, t : t + 1]
                if engines[t] == "S":
                    nc.scalar.activation(out=st[:, t, :], in_=ps[:], func=ACT.Identity, bias=b)
                else:
                    nc.vector.tensor_scalar(out=st[:, t, :], in0=ps[:], scalar1=b, scalar2=None, op0=ALU.add)
            stage[name, c] = st

        def new_inter(name, c):
            inter[name, c] = work.tile([P, CH * T], BF16, name="inter", align_bytes=64)
            return inter[name, c]

        def interleave(name, c, eng):
            it = new_inter(name, c)
            COPY[eng](out=it[:].rearrange("p (n t) -> p n t", t=T), in_=stage[name, c][:].rearrange("p t n -> p n t"))

        def interleave_pe(name, c, engines):
            it = new_inter(name, c)
            for half in range(2):
                src = [stage[name, c][:, :, block(2 * half + i)].rearrange("p t n -> p n t") for i in range(2)]
                via_identity(it[:, banks(2 * half, 2)], src, engines[half])

        def x_quant(name, c):
            quantise(x_q[name][c], inter[name, c])

        sc = {}
        sc_bf = {}
        folded = {}
        neg_max = {}
        e = {}
        e_sum = {}
        inv = {}

        def scores(r, b):
            ps = psum.tile([P, CH], F32, name="ps")
            matmul_mx(ps, x_q["q"][r // 4], block(r % 4), x_q["k"][b])
            nc.vector.tensor_tensor(out=sc[r][:, banks(b, 1)], in0=ps[:], in1=adj_t[r][:, banks(b, 1)], op=ALU.mult)

        def open_row(r):
            sc_r = rows.tile([P, N], F32, name="sc")
            sc[r] = sc_r
            neg_max[r] = stats.tile([P, 2], F32, name="neg_max")

        def cast(r, b, n, eng):
            if b == 0:
                sc_bf[r] = rows.tile([P, N], BF16, name="sc_bf", bufs=3)
            COPY[eng](out=sc_bf[r][:, banks(b, n)], in_=sc[r][:, banks(b, n)])

        def max_of(x, nm):
            nc.vector.tensor_scalar(out=x, in0=x, scalar1=-1.0, scalar2=None, op0=ALU.mult, op1=ALU.min, accum_out=nm)

        def row_max(r):
            max_of(sc_bf[r][:], neg_max[r][:, 0:1])

        def fold(r, half):
            folded[r, half] = work.tile([P, CH], BF16, name="folded", bufs=1)
            a = sc[r][:, banks(2 * half, 1)]
            b = sc[r][:, banks(2 * half + 1, 1)]
            nc.vector.tensor_tensor(out=folded[r, half][:], in0=a, in1=b, op=ALU.max)

        def fold_max(r, half):
            max_of(folded[r, half][:], neg_max[r][:, half : half + 1])

        def row_exp(r, half=None):
            if not half:
                e[r] = rows.tile([P, N], F32, name="e")
                e_sum[r] = stats.tile([P, 2], F32, name="e_sum")
            seg, col = (slice(0, N), 0) if half is None else (banks(2 * half, 2), half)
            nc.scalar.activation(
                out=e[r][:, seg],
                in_=sc[r][:, seg],
                func=ACT.Exp,
                bias=neg_max[r][:, col : col + 1],
                accum_out=e_sum[r][:, col : col + 1],
            )

        def row_recip(r, total=None):
            inv[r] = stats.tile([P, 1], F32, name="inv")
            nc.vector.reciprocal(out=inv[r][:], in_=e_sum[r][:, 0:1] if total is None else total)

        def norm_g(r, b, n):
            x = e[r][:, banks(b, n)]
            nc.gpsimd.tensor_scalar(out=x, in0=x, scalar1=inv[r][:], scalar2=0.0, op0=ALU.mult, op1=ALU.add)

        def norm_v(r, b, n):
            x = e[r][:, banks(b, n)]
            nc.vector.tensor_scalar(out=x, in0=x, scalar1=inv[r][:], scalar2=None, op0=ALU.mult)

        def store(r, b, n):
            nc.sync.dma_start(out=out[r * P : (r + 1) * P, banks(b, n)], in_=e[r][:, banks(b, n)])

        w_copy("k", "V")
        w_quant("k")
        w_copy("q", "S")
        h_mult(0)
        h_turn(0)
        h_mult(1)
        h_quant(0)
        h_turn(1)
        project("k", 0)
        w_quant("q")
        h_mult(2)
        h_quant(1)
        project("q", 0)
        h_mult(3)
        h_turn(2)
        interleave("q", 0, "V")
        interleave_pe("k", 0, "VS")
        h_quant(2)
        x_quant("k", 0)
        h_turn(3)
        x_quant("q", 0)
        project("k", 1, "SVSS")
        h_quant(3)
        project("k", 2, "SVSS")
        for r in range(EARLY):
            open_row(r)
            scores(r, 0)
        interleave("k", 1, "G")
        x_quant("k", 1)
        project("k", 3)
        interleave_pe("k", 2, "SS")
        interleave("k", 3, "V")
        x_quant("k", 2)
        project("q", 1, "SSVS")
        x_quant("k", 3)

        for r in range(ROWS):
            on_g = 4 if r == 0 else 3 if r < 3 else 0 if r >= LAST - 1 else 2 if r % 3 == 1 else 1
            if r >= EARLY:
                open_row(r)
            if r > 1:
                row_exp(r - 2)
            for b in range(4):
                if b > 0 or r >= EARLY:
                    scores(r, b)
                if b < on_g:
                    cast(r, b, 1, "G")
                if r > 0 and b == 3:
                    row_max(r - 1)
                if (r, b) == (0, 0):
                    project("q", 2)
                elif (r, b) == (1, 3):
                    project("q", 3)
                elif (r, b) == (3, 2):
                    interleave_pe("q", 1, "VV")
                    interleave_pe("q", 2, "SS")
                elif (r, b) == (3, 3):
                    x_quant("q", 1)
                    x_quant("q", 2)
                elif (r, b) == (8, 3):
                    interleave_pe("q", 3, "VV")
                elif (r, b) == (9, 3):
                    x_quant("q", 3)
            if r < LAST:
                if on_g < 4:
                    cast(r, on_g, 4 - on_g, "S")
                if r > 1:
                    row_recip(r - 2)
                    norm_g(r - 2, 0, 2)
                    norm_g(r - 2, 2, 2)
                    store(r - 2, 0, 4)
            if r + ADJ_BUFS < ROWS:
                load_adj(r + ADJ_BUFS)

        fold(LAST, 0)
        row_recip(LAST - 2)
        fold_max(LAST, 0)
        norm_v(LAST - 2, 0, 2)
        norm_v(LAST - 2, 2, 2)
        store(LAST - 2, 0, 2)
        row_exp(LAST - 1)
        fold(LAST, 1)
        row_recip(LAST - 1)
        fold_max(LAST, 1)
        norm_v(LAST - 1, 0, 2)
        last_neg = stats.tile([P, 1], F32, name="last_neg")
        nc.vector.tensor_tensor(out=last_neg[:], in0=neg_max[LAST][:, 0:1], in1=neg_max[LAST][:, 1:2], op=ALU.min)
        row_exp(LAST, 0)
        store(LAST - 2, 2, 2)
        norm_v(LAST - 1, 2, 2)
        row_exp(LAST, 1)
        weight = stats.tile([P, 2], F32, name="weight")
        nc.scalar.activation(out=weight[:], in_=neg_max[LAST][:], func=ACT.Exp, scale=-1.0, bias=last_neg[:])
        weighted = stats.tile([P, 2], F32, name="weighted")
        total = stats.tile([P, 1], F32, name="total")
        nc.vector.scalar_tensor_tensor(
            out=weighted[:], in0=e_sum[LAST][:], scalar=1.0, in1=weight[:], op0=ALU.mult, op1=ALU.mult, accum_out=total[:]
        )
        row_recip(LAST, total[:])
        store(LAST - 1, 0, 2)
        store(LAST - 1, 2, 2)
        factor = stats.tile([P, 2], F32, name="factor")
        nc.vector.tensor_scalar(out=factor[:], in0=weight[:], scalar1=inv[LAST][:], scalar2=None, op0=ALU.mult)

        def norm_last(eng, b, n):
            x = e[LAST][:, banks(b, n)]
            col = slice(b // 2, b // 2 + 1)
            if eng == "S":
                nc.scalar.activation(out=x, in_=x, func=ACT.Copy, scale=factor[:, col])
            else:
                nc.vector.tensor_scalar(out=x, in0=x, scalar1=weight[:, col], scalar2=inv[LAST][:], op0=ALU.mult, op1=ALU.mult)

        norm_last("V", 2, 1)
        store(LAST, 2, 1)
        norm_last("S", 3, 1)
        norm_last("V", 0, 2)
        store(LAST, 0, 2)
        store(LAST, 3, 1)
